import numpy as np
import ml_dtypes


def mxq(x, axis, fmt="e4m3"):
    dtype, down = {"e4m3": (ml_dtypes.float8_e4m3fn, 7), "e5m2": (ml_dtypes.float8_e5m2, 14)}[fmt]
    v = np.moveaxis(np.asarray(x, np.float32).astype(ml_dtypes.bfloat16).astype(np.float64), axis, -1)
    blocks = v.reshape(v.shape[:-1] + (-1, 32))
    amax = np.abs(blocks).max(-1, keepdims=True)
    byte = np.maximum(np.where(amax > 0, np.frexp(amax)[1] - 1 + 127, 0) - down, 1)
    scale = np.exp2(byte - 127.0)
    codes = (blocks / scale).astype(np.float32).astype(dtype).astype(np.float64)
    return np.moveaxis((codes * scale).reshape(v.shape), -1, axis)


WIDE = False


def mx_kscale(k):
    if not WIDE:
        return np.ones(k)
    levels = np.array([10, -10, 5, -5, 0])
    a = np.random.permutation(np.resize(levels, k // 512 * 4)).reshape(k // 512, 4)
    idx = np.arange(k)
    return np.exp2(a[idx // 512, idx % 128 // 32])


BF16 = ml_dtypes.bfloat16


def bf(x):
    return np.asarray(x, np.float32).astype(BF16)


def f64(x):
    return np.asarray(x).astype(np.float64)


B, D_IN, H, D_OUT, DEPTH, Q = 512, 1024, 2048, 1024, 3, 2


def quantum_probs(qw):
    n = qw.shape[1]
    s0r, s0i, s1r, s1i = np.ones(n), np.zeros(n), np.zeros(n), np.zeros(n)
    for d in range(qw.shape[0]):
        th = qw[d, :, 0, 0]
        ph = qw[d, :, 1, 1]
        c, s = np.cos(th), np.sin(th)
        n0r, n0i = c * s0r - s * s1r, c * s0i - s * s1i
        n1r, n1i = s * s0r + c * s1r, s * s0i + c * s1i
        cp, sp = np.cos(ph), np.sin(ph)
        s0r, s0i = n0r, n0i
        s1r, s1i = n1r * cp - n1i * sp, n1r * sp + n1i * cp
    return s0r * s0r + s0i * s0i


def setup_inputs():
    s = mx_kscale(H)
    return {"h3": bf(np.maximum(np.random.standard_normal((B, H)), 0.0) * s),
            "q2_qw": bf(np.random.standard_normal((DEPTH, H, Q, Q))),
            "q2_cw": bf(np.random.standard_normal((H, H)) * 1.4 / np.sqrt(H) / s[:, None]),
            "q2_cb": bf(np.random.standard_normal(H) * 0.3),
            "w3": bf(np.random.standard_normal((H, D_OUT)) * 1.4 / np.sqrt(H)),
            "b3": bf(np.random.standard_normal(D_OUT) * 0.3)}


def reference(h3, q2_qw, q2_cw, q2_cb, w3, b3):
    h4 = np.tanh((mxq(f64(h3), 1, "e4m3") @ mxq(f64(q2_cw), 0, "e4m3")) + f64(q2_cb) + quantum_probs(f64(q2_qw))[None, :])
    return np.maximum((mxq(h4, 1, "e4m3") @ mxq(f64(w3), 0, "e4m3")) + f64(b3), 0.0)

@@ -1,0 +1,271 @@
+import math
+from contextlib import ExitStack
+
+import concourse.mybir as mybir
+from concourse.masks import make_identity
+
+F32 = mybir.dt.float32
+BF16 = mybir.dt.bfloat16
+I32 = mybir.dt.int32
+U32 = mybir.dt.uint32
+U8 = mybir.dt.uint8
+FP8X4 = mybir.dt.float8_e4m3fn_x4
+ACT = mybir.ActivationFunctionType
+ALU = mybir.AluOpType
+
+BATCH, HIDDEN, D_OUT, DEPTH = 512, 2048, 1024, 3
+FLOPS = 2 * BATCH * HIDDEN * HIDDEN + 2 * BATCH * HIDDEN * D_OUT
+
+P = 128
+PACK = 4
+K_PASS = P * PACK
+PASSES = HIDDEN // K_PASS
+BANK = 512
+BANKS = 8
+SLICES = HIDDEN // P
+BATCH_SLICES = BATCH // P
+CHUNK = 1024
+CW_CHUNKS = PASSES * (HIDDEN // CHUNK)
+W3_CHUNKS = PASSES * (D_OUT // CHUNK)
+RUN = 4
+VECTOR_COLS = 512
+
+
+def regroup(copy, grouped, rows, cols):
+    copy(
+        out=grouped[:, cols, :].rearrange("p (c i) t -> p c t i", i=RUN),
+        in_=rows[:, :, cols].rearrange("p t (c i) -> p c t i", i=RUN),
+    )
+
+
+def tile_quantumneuralnetwork_pb_kernel(tc, h3, q2_qw, q2_cw, q2_cb, w3, b3, out):
+    nc = tc.nc
+    with ExitStack() as ctx:
+        const = ctx.enter_context(tc.tile_pool(name="const", bufs=1))
+        small = ctx.enter_context(tc.tile_pool(name="small", bufs=2))
+        raw_pool = ctx.enter_context(tc.tile_pool(name="raw", bufs=4))
+        grouped_pool = ctx.enter_context(tc.tile_pool(name="grouped", bufs=3))
+        codes_pool = ctx.enter_context(tc.tile_pool(name="codes", bufs=3))
+        h4_pool = ctx.enter_context(tc.tile_pool(name="h4", bufs=2))
+        out_pool = ctx.enter_context(tc.tile_pool(name="outs", bufs=4))
+        psum = ctx.enter_context(tc.psum_pool(name="psum", bufs=BANKS))
+
+        ident = const.tile([P, P], F32)
+        make_identity(nc, ident[:])
+        ones = const.tile([P, P], BF16)
+        nc.vector.memset(ones[:], 1.0)
+
+        small_rows = const.tile([P, PACK * P], BF16)
+        nc.vector.memset(small_rows[:], 0.0)
+        qw_rows = q2_qw.rearrange("d (s p) a b -> (d s) (p a b)", p=P)
+        nc.sync.dma_start(out=small_rows[0 : DEPTH * SLICES, :], in_=qw_rows)
+        nc.sync.dma_start(out=small_rows[64:96, :], in_=qw_rows[0:32, :])
+        nc.sync.dma_start(out=small_rows[96:112, 0:P], in_=q2_cb.rearrange("(s p) -> s p", p=P))
+        b3_row = const.tile([P, D_OUT], BF16)
+        nc.vector.memset(b3_row[:], 0.0)
+        nc.sync.dma_start(out=b3_row[0:1, :], in_=b3.rearrange("(r o) -> r o", r=1))
+
+        h3_rows = []
+        for i in range(BATCH_SLICES):
+            x = const.tile([P, HIDDEN], BF16, name="h3_rows%d" % i)
+            nc.sync.dma_start(out=x[:], in_=h3[i * P : (i + 1) * P, :])
+            h3_rows.append(x)
+
+        entries = small_rows[:].rearrange("r (p e) -> r p e", e=PACK)
+        picked = const.tile([P, P], F32)
+        nc.vector.tensor_copy(out=picked[0:64, :], in_=entries[0:64, :, 0])
+        nc.vector.tensor_copy(out=picked[64:96, :], in_=entries[64:96, :, 3])
+        nc.vector.tensor_copy(out=picked[96:128, :], in_=small_rows[96:128, 0:P])
+        by_unit = psum.tile([P, BANK], F32, tag="bank")
+        nc.tensor.transpose(by_unit[:, 0:P], picked[:], ident[:])
+        PHI = 64
+        CB = 96
+
+        turns = const.tile([P, 2, CB], F32)
+        for f, quarter in enumerate((0.0, 0.25)):
+            nc.vector.tensor_scalar(
+                out=turns[:, f, :], in0=by_unit[:, 0:CB],
+                scalar1=1.0 / (2.0 * math.pi), scalar2=quarter, op0=ALU.mult, op1=ALU.add,
+            )
+        whole_int = const.tile([P, 2, CB], I32)
+        nc.vector.tensor_copy(out=whole_int[:], in_=turns[:])
+        whole = const.tile([P, 2, CB], F32)
+        nc.vector.tensor_copy(out=whole[:], in_=whole_int[:])
+        rest = const.tile([P, 2, CB], F32)
+        nc.vector.tensor_sub(out=rest[:], in0=turns[:], in1=whole[:])
+        flipped = const.tile([P, 2, CB], F32)
+        nc.vector.scalar_tensor_tensor(
+            out=flipped[:], in0=rest[:], scalar=0.5, in1=rest[:], op0=ALU.is_gt, op1=ALU.subtract
+        )
+        folded = const.tile([P, 2, CB], F32)
+        nc.vector.scalar_tensor_tensor(
+            out=folded[:], in0=flipped[:], scalar=0.5, in1=flipped[:], op0=ALU.is_gt, op1=ALU.subtract
+        )
+        trig = const.tile([P, 2, CB], F32)
+        nc.scalar.activation(out=trig[:], in_=folded[:], func=ACT.Sin, scale=2.0 * math.pi)
+
+        amp = const.tile([P, 2, 2, SLICES], F32)
+        nc.vector.memset(amp[:], 0.0)
+        nc.vector.memset(amp[:, 0, 0, :], 1.0)
+        for d in range(DEPTH):
+            theta = slice(d * SLICES, (d + 1) * SLICES)
+            by_sin = small.tile([P, 2, 2, SLICES], F32)
+            by_cos = small.tile([P, 2, 2, SLICES], F32)
+            for f, product in enumerate((by_sin, by_cos)):
+                nc.vector.tensor_mul(
+                    out=product[:].rearrange("p a c s -> p (a c) s"),
+                    in0=amp[:].rearrange("p a c s -> p (a c) s"),
+                    in1=trig[:, f, theta].unsqueeze(1).to_broadcast([P, 4, SLICES]),
+                )
+            turned = small.tile([P, 2, 2, SLICES], F32)
+            nc.vector.tensor_sub(out=turned[:, 0], in0=by_cos[:, 0], in1=by_sin[:, 1])
+            nc.vector.tensor_add(out=turned[:, 1], in0=by_sin[:, 0], in1=by_cos[:, 1])
+            if d < DEPTH - 1:
+                phi = slice(PHI + d * SLICES, PHI + (d + 1) * SLICES)
+                ph_sin = small.tile([P, 2, SLICES], F32)
+                ph_cos = small.tile([P, 2, SLICES], F32)
+                for f, product in enumerate((ph_sin, ph_cos)):
+                    nc.vector.tensor_mul(
+                        out=product[:],
+                        in0=turned[:, 1],
+                        in1=trig[:, f, phi].unsqueeze(1).to_broadcast([P, 2, SLICES]),
+                    )
+                nc.vector.tensor_sub(out=turned[:, 1, 0, :], in0=ph_cos[:, 0, :], in1=ph_sin[:, 1, :])
+                nc.vector.tensor_add(out=turned[:, 1, 1, :], in0=ph_sin[:, 0, :], in1=ph_cos[:, 1, :])
+            amp = turned
+        squares = small.tile([P, 2, SLICES], F32)
+        nc.vector.tensor_mul(out=squares[:], in0=amp[:, 0], in1=amp[:, 0])
+        prob = small.tile([P, SLICES], F32)
+        nc.vector.tensor_add(out=prob[:], in0=squares[:, 0, :], in1=squares[:, 1, :])
+        hidden_bias = const.tile([P, SLICES], F32)
+        nc.vector.tensor_add(out=hidden_bias[:], in0=prob[:], in1=by_unit[:, CB : CB + SLICES])
+
+        b3_all = const.tile([P, D_OUT], F32)
+        for o in range(D_OUT // BANK):
+            cols = slice(o * BANK, (o + 1) * BANK)
+            spread = psum.tile([P, BANK], F32, tag="bank")
+            nc.tensor.matmul(out=spread[:], lhsT=ones[:], rhs=b3_row[:, cols], start=True, stop=True)
+            nc.scalar.copy(out=b3_all[:, cols], in_=spread[:])
+
+        h3_grouped = const.tile([P, PASSES * BATCH * PACK], BF16, align_bytes=64)
+        h3_grouped_words = h3_grouped[:].bitcast(F32).rearrange("q (g b u) -> q g b u", g=PASSES, u=2)
+        for i in range(BATCH_SLICES):
+            words = h3_rows[i][:].bitcast(F32)
+            for pair in range(PASSES // 2):
+                flipped_words = psum.tile([P, BANK], F32, tag="bank")
+                for j in range(4):
+                    block = 4 * pair + j
+                    nc.tensor.transpose(
+                        flipped_words[:, j * P : (j + 1) * P], words[:, block * P : (block + 1) * P], ident[:]
+                    )
+                nc.scalar.copy(
+                    out=h3_grouped_words[:, 2 * pair : 2 * pair + 2, i * P : (i + 1) * P, :],
+                    in_=flipped_words[:].rearrange("q (g u b) -> q g b u", g=2, u=2),
+                )
+        h3_codes = const.tile([P, PASSES * BATCH], U32, align_bytes=64)
+        h3_scales = const.tile([P, PASSES * BATCH], U8, align_bytes=64)
+        for g in range(PASSES):
+            nc.vector.quantize_mx(
+                out=h3_codes[:, g * BATCH : (g + 1) * BATCH].bitcast(FP8X4),
+                scales=h3_scales[:, g * BATCH : (g + 1) * BATCH],
+                in_=h3_grouped[:, g * BATCH * PACK : (g + 1) * BATCH * PACK],
+            )
+
+        h4_codes = const.tile([P, PASSES * BATCH], U32, align_bytes=64)
+        h4_scales = const.tile([P, PASSES * BATCH], U8, align_bytes=64)
+        staged = {}
+        sums = {}
+
+        def stage_in(c):
+            raw = raw_pool.tile([P, PACK, CHUNK], BF16, name="raw")
+            if c < CW_CHUNKS:
+                half, g = divmod(c, PASSES)
+                for u in range(2):
+                    first = g * K_PASS + u * 2 * P
+                    nc.sync.dma_start(
+                        out=raw[:, 2 * u : 2 * u + 2, :],
+                        in_=q2_cw[first : first + 2 * P, half * CHUNK : (half + 1) * CHUNK].rearrange(
+                            "(q e) n -> q e n", e=2
+                        ),
+                    )
+            else:
+                g = c - CW_CHUNKS
+                nc.sync.dma_start(
+                    out=raw[:], in_=w3[g * K_PASS : (g + 1) * K_PASS, :].rearrange("(t q) o -> q t o", t=PACK)
+                )
+            grouped = grouped_pool.tile([P, CHUNK, PACK], BF16, name="grouped", align_bytes=64)
+            regroup(nc.vector.tensor_copy, grouped, raw, slice(0, VECTOR_COLS))
+            regroup(nc.scalar.copy, grouped, raw, slice(VECTOR_COLS, CHUNK))
+            staged[c] = grouped
+
+        def quantise_chunk(c):
+            codes = codes_pool.tile([P, CHUNK], U32, name="codes", align_bytes=64)
+            scales = codes_pool.tile([P, CHUNK], U8, name="scales", align_bytes=64)
+            nc.vector.quantize_mx(
+                out=codes[:].bitcast(FP8X4), scales=scales[:], in_=staged[c][:].rearrange("p c t -> p (c t)")
+            )
+            return codes, scales
+
+        def first_product(c):
+            half, g = divmod(c, PASSES)
+            codes, scales = quantise_chunk(c)
+            if g == 0:
+                for s in range(BANKS):
+                    sums[s] = psum.tile([P, BANK], F32, tag="bank", name="hidden_sum%d" % s)
+            batch = slice(g * BATCH, (g + 1) * BATCH)
+            for s in range(BANKS):
+                units = slice(s * P, (s + 1) * P)
+                nc.tensor.matmul_mx(
+                    out=sums[s][:],
+                    lhsT=codes[:, units].bitcast(FP8X4), lhsT_scale=scales[:, units],
+                    rhs=h3_codes[:, batch].bitcast(FP8X4), rhs_scale=h3_scales[:, batch],
+                    start=(g == 0), stop=(g == PASSES - 1),
+                )
+            if g < PASSES - 1:
+                return
+            for local in range(BANKS // PACK):
+                g2 = half * (BANKS // PACK) + local
+                h4_rows = h4_pool.tile([P, PACK, BATCH], BF16, name="h4_rows")
+                for t in range(PACK):
+                    s = local * PACK + t
+                    nc.scalar.activation(
+                        out=h4_rows[:, t, :], in_=sums[s][:], func=ACT.Tanh,
+                        bias=hidden_bias[:, half * BANKS + s : half * BANKS + s + 1], scale=1.0,
+                    )
+                h4_grouped = h4_pool.tile([P, BATCH, PACK], BF16, name="h4_grouped", align_bytes=64)
+                regroup(nc.vector.tensor_copy, h4_grouped, h4_rows, slice(0, BATCH))
+                nc.vector.quantize_mx(
+                    out=h4_codes[:, g2 * BATCH : (g2 + 1) * BATCH].bitcast(FP8X4),
+                    scales=h4_scales[:, g2 * BATCH : (g2 + 1) * BATCH],
+                    in_=h4_grouped[:].rearrange("p b t -> p (b t)"),
+                )
+
+        def second_product(c):
+            g = c - CW_CHUNKS
+            codes, scales = quantise_chunk(c)
+            for i in range(BATCH_SLICES):
+                rows = slice(g * BATCH + i * P, g * BATCH + (i + 1) * P)
+                for o in range(D_OUT // BANK):
+                    cols = slice(o * BANK, (o + 1) * BANK)
+                    if g == 0:
+                        sums[(i, o)] = psum.tile([P, BANK], F32, tag="bank", name="out_sum%d%d" % (i, o))
+                    nc.tensor.matmul_mx(
+                        out=sums[(i, o)][:],
+                        lhsT=h4_codes[:, rows].bitcast(FP8X4), lhsT_scale=h4_scales[:, rows],
+                        rhs=codes[:, cols].bitcast(FP8X4), rhs_scale=scales[:, cols],
+                        start=(g == 0), stop=(g == PASSES - 1),
+                    )
+                    if g == PASSES - 1:
+                        result = out_pool.tile([P, BANK], F32, name="result")
+                        nc.vector.tensor_add(out=result[:], in0=sums[(i, o)][:], in1=b3_all[:, cols])
+                        nc.scalar.activation(out=result[:], in_=result[:], func=ACT.Relu)
+                        nc.sync.dma_start(out=out[i * P : (i + 1) * P, cols], in_=result[:])
+
+        stage_in(0)
+        for c in range(CW_CHUNKS + W3_CHUNKS):
+            if c + 1 < CW_CHUNKS + W3_CHUNKS:
+                stage_in(c + 1)
+            if c < CW_CHUNKS:
+                first_product(c)
+            else:
+                second_product(c)

@@ -28,13 +28,12 @@ CHUNK = 1024
 CW_CHUNKS = PASSES * (HIDDEN // CHUNK)
 W3_CHUNKS = PASSES * (D_OUT // CHUNK)
 RUN = 4
-VECTOR_COLS = 512
 
 
-def regroup(copy, grouped, rows, cols):
+def regroup(copy, grouped, rows):
     copy(
-        out=grouped[:, cols, :].rearrange("p (c i) t -> p c t i", i=RUN),
-        in_=rows[:, :, cols].rearrange("p t (c i) -> p c t i", i=RUN),
+        out=grouped.rearrange("p (c i) t -> p c t i", i=RUN),
+        in_=rows.rearrange("p t (c i) -> p c t i", i=RUN),
     )
 
 
@@ -43,7 +42,7 @@ def tile_quantumneuralnetwork_pb_kernel(tc, h3, q2_qw, q2_cw, q2_cb, w3, b3, out
     with ExitStack() as ctx:
         const = ctx.enter_context(tc.tile_pool(name="const", bufs=1))
         small = ctx.enter_context(tc.tile_pool(name="small", bufs=2))
-        raw_pool = ctx.enter_context(tc.tile_pool(name="raw", bufs=4))
+        raw_pool = ctx.enter_context(tc.tile_pool(name="raw", bufs=CW_CHUNKS))
         grouped_pool = ctx.enter_context(tc.tile_pool(name="grouped", bufs=3))
         codes_pool = ctx.enter_context(tc.tile_pool(name="codes", bufs=3))
         h4_pool = ctx.enter_context(tc.tile_pool(name="h4", bufs=2))
@@ -52,8 +51,6 @@ def tile_quantumneuralnetwork_pb_kernel(tc, h3, q2_qw, q2_cw, q2_cb, w3, b3, out
 
         ident = const.tile([P, P], F32)
         make_identity(nc, ident[:])
-        ones = const.tile([P, P], BF16)
-        nc.vector.memset(ones[:], 1.0)
 
         small_rows = const.tile([P, PACK * P], BF16)
         nc.vector.memset(small_rows[:], 0.0)
@@ -61,15 +58,35 @@ def tile_quantumneuralnetwork_pb_kernel(tc, h3, q2_qw, q2_cw, q2_cb, w3, b3, out
         nc.sync.dma_start(out=small_rows[0 : DEPTH * SLICES, :], in_=qw_rows)
         nc.sync.dma_start(out=small_rows[64:96, :], in_=qw_rows[0:32, :])
         nc.sync.dma_start(out=small_rows[96:112, 0:P], in_=q2_cb.rearrange("(s p) -> s p", p=P))
-        b3_row = const.tile([P, D_OUT], BF16)
-        nc.vector.memset(b3_row[:], 0.0)
-        nc.sync.dma_start(out=b3_row[0:1, :], in_=b3.rearrange("(r o) -> r o", r=1))
 
         h3_rows = []
         for i in range(BATCH_SLICES):
             x = const.tile([P, HIDDEN], BF16, name="h3_rows%d" % i)
             nc.sync.dma_start(out=x[:], in_=h3[i * P : (i + 1) * P, :])
             h3_rows.append(x)
+
+        raw = {}
+
+        def load(c):
+            raw[c] = raw_pool.tile([P, PACK, CHUNK], BF16, name="raw")
+            if c < CW_CHUNKS:
+                half, g = divmod(c, PASSES)
+                for u in range(2):
+                    first = g * K_PASS + u * 2 * P
+                    nc.sync.dma_start(
+                        out=raw[c][:, 2 * u : 2 * u + 2, :],
+                        in_=q2_cw[first : first + 2 * P, half * CHUNK : (half + 1) * CHUNK].rearrange(
+                            "(q e) n -> q e n", e=2
+                        ),
+                    )
+            else:
+                g = c - CW_CHUNKS
+                nc.sync.dma_start(
+                    out=raw[c][:], in_=w3[g * K_PASS : (g + 1) * K_PASS, :].rearrange("(t q) o -> q t o", t=PACK)
+                )
+
+        for c in range(CW_CHUNKS):
+            load(c)
 
         entries = small_rows[:].rearrange("r (p e) -> r p e", e=PACK)
         picked = const.tile([P, P], F32)
@@ -103,6 +120,8 @@ def tile_quantumneuralnetwork_pb_kernel(tc, h3, q2_qw, q2_cw, q2_cb, w3, b3, out
         )
         trig = const.tile([P, 2, CB], F32)
         nc.scalar.activation(out=trig[:], in_=folded[:], func=ACT.Sin, scale=2.0 * math.pi)
+        table_warmer = const.tile([P, 1], F32)
+        nc.scalar.activation(out=table_warmer[:], in_=trig[:, 0, 0:1], func=ACT.Tanh)
 
         amp = const.tile([P, 2, 2, SLICES], F32)
         nc.vector.memset(amp[:], 0.0)
@@ -140,13 +159,6 @@ def tile_quantumneuralnetwork_pb_kernel(tc, h3, q2_qw, q2_cw, q2_cb, w3, b3, out
         hidden_bias = const.tile([P, SLICES], F32)
         nc.vector.tensor_add(out=hidden_bias[:], in0=prob[:], in1=by_unit[:, CB : CB + SLICES])
 
-        b3_all = const.tile([P, D_OUT], F32)
-        for o in range(D_OUT // BANK):
-            cols = slice(o * BANK, (o + 1) * BANK)
-            spread = psum.tile([P, BANK], F32, tag="bank")
-            nc.tensor.matmul(out=spread[:], lhsT=ones[:], rhs=b3_row[:, cols], start=True, stop=True)
-            nc.scalar.copy(out=b3_all[:, cols], in_=spread[:])
-
         h3_grouped = const.tile([P, PASSES * BATCH * PACK], BF16, align_bytes=64)
         h3_grouped_words = h3_grouped[:].bitcast(F32).rearrange("q (g b u) -> q g b u", g=PASSES, u=2)
         for i in range(BATCH_SLICES):
@@ -158,7 +170,8 @@ def tile_quantumneuralnetwork_pb_kernel(tc, h3, q2_qw, q2_cw, q2_cb, w3, b3, out
                     nc.tensor.transpose(
                         flipped_words[:, j * P : (j + 1) * P], words[:, block * P : (block + 1) * P], ident[:]
                     )
-                nc.scalar.copy(
+                copy = (nc.scalar.copy, nc.vector.tensor_copy)[pair]
+                copy(
                     out=h3_grouped_words[:, 2 * pair : 2 * pair + 2, i * P : (i + 1) * P, :],
                     in_=flipped_words[:].rearrange("q (g u b) -> q g b u", g=2, u=2),
                 )
@@ -171,101 +184,117 @@ def tile_quantumneuralnetwork_pb_kernel(tc, h3, q2_qw, q2_cw, q2_cb, w3, b3, out
                 in_=h3_grouped[:, g * BATCH * PACK : (g + 1) * BATCH * PACK],
             )
 
+        units = [("cw", half, g) for half in range(HIDDEN // CHUNK) for g in range(PASSES)]
+        units += [("w3", o, g) for o in range(D_OUT // BANK) for g in range(PASSES)]
         h4_codes = const.tile([P, PASSES * BATCH], U32, align_bytes=64)
         h4_scales = const.tile([P, PASSES * BATCH], U8, align_bytes=64)
+        b3_all = const.tile([P, D_OUT], BF16)
         staged = {}
         sums = {}
 
-        def stage_in(c):
-            raw = raw_pool.tile([P, PACK, CHUNK], BF16, name="raw")
-            if c < CW_CHUNKS:
-                half, g = divmod(c, PASSES)
-                for u in range(2):
-                    first = g * K_PASS + u * 2 * P
-                    nc.sync.dma_start(
-                        out=raw[:, 2 * u : 2 * u + 2, :],
-                        in_=q2_cw[first : first + 2 * P, half * CHUNK : (half + 1) * CHUNK].rearrange(
-                            "(q e) n -> q e n", e=2
-                        ),
-                    )
+        def stage_in(n):
+            kind, part, g = units[n]
+            if kind == "cw":
+                rows = raw[part * PASSES + g][:]
             else:
-                g = c - CW_CHUNKS
-                nc.sync.dma_start(
-                    out=raw[:], in_=w3[g * K_PASS : (g + 1) * K_PASS, :].rearrange("(t q) o -> q t o", t=PACK)
-                )
-            grouped = grouped_pool.tile([P, CHUNK, PACK], BF16, name="grouped", align_bytes=64)
-            regroup(nc.vector.tensor_copy, grouped, raw, slice(0, VECTOR_COLS))
-            regroup(nc.scalar.copy, grouped, raw, slice(VECTOR_COLS, CHUNK))
-            staged[c] = grouped
+                rows = raw[CW_CHUNKS + g][:, :, part * BANK : (part + 1) * BANK]
+            width = rows.shape[2]
+            grouped = grouped_pool.tile([P, width, PACK], BF16, name="grouped", align_bytes=64)
+            regroup(nc.vector.tensor_copy, grouped[:, 0 : width // 2, :], rows[:, :, 0 : width // 2])
+            regroup(nc.scalar.copy, grouped[:, width // 2 : width, :], rows[:, :, width // 2 : width])
+            staged[n] = grouped
+            if n < W3_CHUNKS:
+                load(CW_CHUNKS + n)
+            if n == W3_CHUNKS:
+                nc.sync.dma_start(out=b3_all[:], in_=b3.partition_broadcast(P))
 
-        def quantise_chunk(c):
-            codes = codes_pool.tile([P, CHUNK], U32, name="codes", align_bytes=64)
-            scales = codes_pool.tile([P, CHUNK], U8, name="scales", align_bytes=64)
+        def quantise_unit(n):
+            width = staged[n].shape[1]
+            codes = codes_pool.tile([P, width], U32, name="codes", align_bytes=64)
+            scales = codes_pool.tile([P, width], U8, name="scales", align_bytes=64)
             nc.vector.quantize_mx(
-                out=codes[:].bitcast(FP8X4), scales=scales[:], in_=staged[c][:].rearrange("p c t -> p (c t)")
+                out=codes[:].bitcast(FP8X4), scales=scales[:], in_=staged[n][:].rearrange("p c t -> p (c t)")
             )
             return codes, scales
 
-        def first_product(c):
-            half, g = divmod(c, PASSES)
-            codes, scales = quantise_chunk(c)
-            if g == 0:
+        def multiply(n):
+            kind, part, g = units[n]
+            codes, scales = quantise_unit(n)
+            first, last = g == 0, g == PASSES - 1
+            if kind == "cw":
+                batch = slice(g * BATCH, (g + 1) * BATCH)
                 for s in range(BANKS):
-                    sums[s] = psum.tile([P, BANK], F32, tag="bank", name="hidden_sum%d" % s)
-            batch = slice(g * BATCH, (g + 1) * BATCH)
-            for s in range(BANKS):
-                units = slice(s * P, (s + 1) * P)
-                nc.tensor.matmul_mx(
-                    out=sums[s][:],
-                    lhsT=codes[:, units].bitcast(FP8X4), lhsT_scale=scales[:, units],
-                    rhs=h3_codes[:, batch].bitcast(FP8X4), rhs_scale=h3_scales[:, batch],
-                    start=(g == 0), stop=(g == PASSES - 1),
-                )
-            if g < PASSES - 1:
-                return
-            for local in range(BANKS // PACK):
-                g2 = half * (BANKS // PACK) + local
-                h4_rows = h4_pool.tile([P, PACK, BATCH], BF16, name="h4_rows")
-                for t in range(PACK):
-                    s = local * PACK + t
-                    nc.scalar.activation(
-                        out=h4_rows[:, t, :], in_=sums[s][:], func=ACT.Tanh,
-                        bias=hidden_bias[:, half * BANKS + s : half * BANKS + s + 1], scale=1.0,
-                    )
-                h4_grouped = h4_pool.tile([P, BATCH, PACK], BF16, name="h4_grouped", align_bytes=64)
-                regroup(nc.vector.tensor_copy, h4_grouped, h4_rows, slice(0, BATCH))
-                nc.vector.quantize_mx(
-                    out=h4_codes[:, g2 * BATCH : (g2 + 1) * BATCH].bitcast(FP8X4),
-                    scales=h4_scales[:, g2 * BATCH : (g2 + 1) * BATCH],
-                    in_=h4_grouped[:].rearrange("p b t -> p (b t)"),
-                )
-
-        def second_product(c):
-            g = c - CW_CHUNKS
-            codes, scales = quantise_chunk(c)
-            for i in range(BATCH_SLICES):
-                rows = slice(g * BATCH + i * P, g * BATCH + (i + 1) * P)
-                for o in range(D_OUT // BANK):
-                    cols = slice(o * BANK, (o + 1) * BANK)
-                    if g == 0:
-                        sums[(i, o)] = psum.tile([P, BANK], F32, tag="bank", name="out_sum%d%d" % (i, o))
+                    if first:
+                        sums[s] = psum.tile([P, BANK], F32, tag="bank", name="hidden_sum%d" % s)
+                    cols = slice(s * P, (s + 1) * P)
                     nc.tensor.matmul_mx(
-                        out=sums[(i, o)][:],
-                        lhsT=h4_codes[:, rows].bitcast(FP8X4), lhsT_scale=h4_scales[:, rows],
-                        rhs=codes[:, cols].bitcast(FP8X4), rhs_scale=scales[:, cols],
-                        start=(g == 0), stop=(g == PASSES - 1),
+                        out=sums[s][:],
+                        lhsT=codes[:, cols].bitcast(FP8X4), lhsT_scale=scales[:, cols],
+                        rhs=h3_codes[:, batch].bitcast(FP8X4), rhs_scale=h3_scales[:, batch],
+                        start=first, stop=last,
                     )
-                    if g == PASSES - 1:
-                        result = out_pool.tile([P, BANK], F32, name="result")
-                        nc.vector.tensor_add(out=result[:], in0=sums[(i, o)][:], in1=b3_all[:, cols])
-                        nc.scalar.activation(out=result[:], in_=result[:], func=ACT.Relu)
-                        nc.sync.dma_start(out=out[i * P : (i + 1) * P, cols], in_=result[:])
-
-        stage_in(0)
-        for c in range(CW_CHUNKS + W3_CHUNKS):
-            if c + 1 < CW_CHUNKS + W3_CHUNKS:
-                stage_in(c + 1)
-            if c < CW_CHUNKS:
-                first_product(c)
             else:
-                second_product(c)
+                for i in range(BATCH_SLICES):
+                    if first:
+                        sums[(part, i)] = psum.tile([P, BANK], F32, tag="bank", name="out_sum%d" % i)
+                    rows = slice(g * BATCH + i * P, g * BATCH + (i + 1) * P)
+                    nc.tensor.matmul_mx(
+                        out=sums[(part, i)][:],
+                        lhsT=h4_codes[:, rows].bitcast(FP8X4), lhsT_scale=h4_scales[:, rows],
+                        rhs=codes[:].bitcast(FP8X4), rhs_scale=scales[:],
+                        start=first, stop=last,
+                    )
+
+        h4_rows = {}
+
+        def tanh_half(half):
+            for s in range(BANKS):
+                g2, t = divmod(half * BANKS + s, PACK)
+                if t == 0:
+                    h4_rows[g2] = h4_pool.tile([P, PACK, BATCH], BF16, name="h4_rows")
+                nc.scalar.activation(
+                    out=h4_rows[g2][:, t, :], in_=sums[s][:], func=ACT.Tanh,
+                    bias=hidden_bias[:, half * BANKS + s : half * BANKS + s + 1], scale=1.0,
+                )
+
+        def quantise_h4(g2):
+            h4_grouped = h4_pool.tile([P, BATCH, PACK], BF16, name="h4_grouped", align_bytes=64)
+            regroup(nc.vector.tensor_copy, h4_grouped[:], h4_rows[g2][:])
+            nc.vector.quantize_mx(
+                out=h4_codes[:, g2 * BATCH : (g2 + 1) * BATCH].bitcast(FP8X4),
+                scales=h4_scales[:, g2 * BATCH : (g2 + 1) * BATCH],
+                in_=h4_grouped[:].rearrange("p b t -> p (b t)"),
+            )
+
+        results = {}
+
+        def add_b3(o):
+            for i in range(BATCH_SLICES):
+                results[i] = out_pool.tile([P, BANK], F32, name="result")
+                nc.vector.tensor_add(
+                    out=results[i][:], in0=sums[(o, i)][:], in1=b3_all[:, o * BANK : (o + 1) * BANK]
+                )
+
+        def relu_and_store(o):
+            for i in range(BATCH_SLICES):
+                nc.scalar.activation(out=results[i][:], in_=results[i][:], func=ACT.Relu)
+                nc.sync.dma_start(out=out[i * P : (i + 1) * P, o * BANK : (o + 1) * BANK], in_=results[i][:])
+
+        def closes(n, kind):
+            return 0 <= n < len(units) and units[n][0] == kind and units[n][2] == PASSES - 1
+
+        for n in range(-1, len(units) + 2):
+            if n + 1 < len(units):
+                stage_in(n + 1)
+            if closes(n - 1, "cw"):
+                tanh_half(units[n - 1][1])
+            if closes(n - 2, "cw"):
+                quantise_h4(2 * units[n - 2][1])
+            if closes(n - 3, "cw"):
+                quantise_h4(2 * units[n - 3][1] + 1)
+            if closes(n - 1, "w3"):
+                add_b3(units[n - 1][1])
+            if closes(n - 2, "w3"):
+                relu_and_store(units[n - 2][1])
+            if 0 <= n < len(units):
+                multiply(n)

@@ -28,6 +28,7 @@ CHUNK = 1024
 CW_CHUNKS = PASSES * (HIDDEN // CHUNK)
 W3_CHUNKS = PASSES * (D_OUT // CHUNK)
 RUN = 4
+VECTOR_SIXTEENTHS = 8
 
 
 def regroup(copy, grouped, rows):
@@ -46,7 +47,7 @@ def tile_quantumneuralnetwork_pb_kernel(tc, h3, q2_qw, q2_cw, q2_cb, w3, b3, out
         grouped_pool = ctx.enter_context(tc.tile_pool(name="grouped", bufs=3))
         codes_pool = ctx.enter_context(tc.tile_pool(name="codes", bufs=3))
         h4_pool = ctx.enter_context(tc.tile_pool(name="h4", bufs=2))
-        out_pool = ctx.enter_context(tc.tile_pool(name="outs", bufs=4))
+        out_pool = ctx.enter_context(tc.tile_pool(name="outs", bufs=8))
         psum = ctx.enter_context(tc.psum_pool(name="psum", bufs=BANKS))
 
         ident = const.tile([P, P], F32)
@@ -58,12 +59,6 @@ def tile_quantumneuralnetwork_pb_kernel(tc, h3, q2_qw, q2_cw, q2_cb, w3, b3, out
         nc.sync.dma_start(out=small_rows[0 : DEPTH * SLICES, :], in_=qw_rows)
         nc.sync.dma_start(out=small_rows[64:96, :], in_=qw_rows[0:32, :])
         nc.sync.dma_start(out=small_rows[96:112, 0:P], in_=q2_cb.rearrange("(s p) -> s p", p=P))
-
-        h3_rows = []
-        for i in range(BATCH_SLICES):
-            x = const.tile([P, HIDDEN], BF16, name="h3_rows%d" % i)
-            nc.sync.dma_start(out=x[:], in_=h3[i * P : (i + 1) * P, :])
-            h3_rows.append(x)
 
         raw = {}
 
@@ -85,8 +80,49 @@ def tile_quantumneuralnetwork_pb_kernel(tc, h3, q2_qw, q2_cw, q2_cb, w3, b3, out
                     out=raw[c][:], in_=w3[g * K_PASS : (g + 1) * K_PASS, :].rearrange("(t q) o -> q t o", t=PACK)
                 )
 
-        for c in range(CW_CHUNKS):
+        for c in range(0):
             load(c)
+        h3_rows = []
+        for i in range(BATCH_SLICES):
+            x = const.tile([P, HIDDEN], BF16, name="h3_rows%d" % i)
+            nc.sync.dma_start(out=x[:], in_=h3[i * P : (i + 1) * P, :])
+            h3_rows.append(x)
+        for c in range(0, CW_CHUNKS):
+            load(c)
+
+        units = [("cw", half, g) for half in range(HIDDEN // CHUNK) for g in range(PASSES)]
+        units += [("w3", o, g) for o in range(D_OUT // BANK) for g in range(PASSES)]
+        b3_all = const.tile([P, D_OUT], BF16)
+        staged = {}
+
+        def stage_in(n):
+            kind, part, g = units[n]
+            if kind == "cw":
+                rows = raw[part * PASSES + g][:]
+            else:
+                rows = raw[CW_CHUNKS + g][:, :, part * BANK : (part + 1) * BANK]
+            width = rows.shape[2]
+            split = width * VECTOR_SIXTEENTHS // 16
+            grouped = grouped_pool.tile([P, width, PACK], BF16, name="grouped", align_bytes=64)
+            regroup(nc.vector.tensor_copy, grouped[:, 0:split, :], rows[:, :, 0:split])
+            regroup(nc.scalar.copy, grouped[:, split:width, :], rows[:, :, split:width])
+            staged[n] = grouped
+            if n < W3_CHUNKS:
+                load(CW_CHUNKS + n)
+            if n == W3_CHUNKS:
+                nc.sync.dma_start(out=b3_all[:], in_=b3.partition_broadcast(P))
+
+        def quantise_unit(n):
+            width = staged[n].shape[1]
+            codes = codes_pool.tile([P, width], U32, name="codes", align_bytes=64)
+            scales = codes_pool.tile([P, width], U8, name="scales", align_bytes=64)
+            nc.vector.quantize_mx(
+                out=codes[:].bitcast(FP8X4), scales=scales[:], in_=staged[n][:].rearrange("p c t -> p (c t)")
+            )
+            return codes, scales
+
+        for n in range(0):
+            stage_in(n)
 
         entries = small_rows[:].rearrange("r (p e) -> r p e", e=PACK)
         picked = const.tile([P, P], F32)
@@ -184,38 +220,9 @@ def tile_quantumneuralnetwork_pb_kernel(tc, h3, q2_qw, q2_cw, q2_cb, w3, b3, out
                 in_=h3_grouped[:, g * BATCH * PACK : (g + 1) * BATCH * PACK],
             )
 
-        units = [("cw", half, g) for half in range(HIDDEN // CHUNK) for g in range(PASSES)]
-        units += [("w3", o, g) for o in range(D_OUT // BANK) for g in range(PASSES)]
         h4_codes = const.tile([P, PASSES * BATCH], U32, align_bytes=64)
         h4_scales = const.tile([P, PASSES * BATCH], U8, align_bytes=64)
-        b3_all = const.tile([P, D_OUT], BF16)
-        staged = {}
         sums = {}
-
-        def stage_in(n):
-            kind, part, g = units[n]
-            if kind == "cw":
-                rows = raw[part * PASSES + g][:]
-            else:
-                rows = raw[CW_CHUNKS + g][:, :, part * BANK : (part + 1) * BANK]
-            width = rows.shape[2]
-            grouped = grouped_pool.tile([P, width, PACK], BF16, name="grouped", align_bytes=64)
-            regroup(nc.vector.tensor_copy, grouped[:, 0 : width // 2, :], rows[:, :, 0 : width // 2])
-            regroup(nc.scalar.copy, grouped[:, width // 2 : width, :], rows[:, :, width // 2 : width])
-            staged[n] = grouped
-            if n < W3_CHUNKS:
-                load(CW_CHUNKS + n)
-            if n == W3_CHUNKS:
-                nc.sync.dma_start(out=b3_all[:], in_=b3.partition_broadcast(P))
-
-        def quantise_unit(n):
-            width = staged[n].shape[1]
-            codes = codes_pool.tile([P, width], U32, name="codes", align_bytes=64)
-            scales = codes_pool.tile([P, width], U8, name="scales", align_bytes=64)
-            nc.vector.quantize_mx(
-                out=codes[:].bitcast(FP8X4), scales=scales[:], in_=staged[n][:].rearrange("p c t -> p (c t)")
-            )
-            return codes, scales
 
         def multiply(n):
             kind, part, g = units[n]
@@ -270,20 +277,22 @@ def tile_quantumneuralnetwork_pb_kernel(tc, h3, q2_qw, q2_cw, q2_cb, w3, b3, out
 
         def add_b3(o):
             for i in range(BATCH_SLICES):
-                results[i] = out_pool.tile([P, BANK], F32, name="result")
+                results[(o, i)] = out_pool.tile([P, BANK], F32, name="result")
                 nc.vector.tensor_add(
-                    out=results[i][:], in0=sums[(o, i)][:], in1=b3_all[:, o * BANK : (o + 1) * BANK]
+                    out=results[(o, i)][:], in0=sums[(o, i)][:], in1=b3_all[:, o * BANK : (o + 1) * BANK]
                 )
 
         def relu_and_store(o):
             for i in range(BATCH_SLICES):
-                nc.scalar.activation(out=results[i][:], in_=results[i][:], func=ACT.Relu)
-                nc.sync.dma_start(out=out[i * P : (i + 1) * P, o * BANK : (o + 1) * BANK], in_=results[i][:])
+                nc.scalar.activation(out=results[(o, i)][:], in_=results[(o, i)][:], func=ACT.Relu)
+                nc.sync.dma_start(
+                    out=out[i * P : (i + 1) * P, o * BANK : (o + 1) * BANK], in_=results[(o, i)][:]
+                )
 
         def closes(n, kind):
             return 0 <= n < len(units) and units[n][0] == kind and units[n][2] == PASSES - 1
 
-        for n in range(-1, len(units) + 2):
+        for n in range(0 - 1, len(units) + 2):
             if n + 1 < len(units):
                 stage_in(n + 1)
             if closes(n - 1, "cw"):
@@ -292,9 +301,10 @@ def tile_quantumneuralnetwork_pb_kernel(tc, h3, q2_qw, q2_cw, q2_cb, w3, b3, out
                 quantise_h4(2 * units[n - 2][1])
             if closes(n - 3, "cw"):
                 quantise_h4(2 * units[n - 3][1] + 1)
-            if closes(n - 1, "w3"):
-                add_b3(units[n - 1][1])
-            if closes(n - 2, "w3"):
-                relu_and_store(units[n - 2][1])
             if 0 <= n < len(units):
                 multiply(n)
+            if n == len(units) - 1:
+                for o in range(D_OUT // BANK):
+                    add_b3(o)
+                for o in range(D_OUT // BANK):
+                    relu_and_store(o)

@@ -28,7 +28,8 @@ CHUNK = 1024
 CW_CHUNKS = PASSES * (HIDDEN // CHUNK)
 W3_CHUNKS = PASSES * (D_OUT // CHUNK)
 RUN = 4
-VECTOR_SIXTEENTHS = 8
+FLIP = [0] * 16
+VECTOR = [544] * 8 + [272] * 8
 
 
 def regroup(copy, grouped, rows):
@@ -50,15 +51,24 @@ def tile_quantumneuralnetwork_pb_kernel(tc, h3, q2_qw, q2_cw, q2_cb, w3, b3, out
         out_pool = ctx.enter_context(tc.tile_pool(name="outs", bufs=8))
         psum = ctx.enter_context(tc.psum_pool(name="psum", bufs=BANKS))
 
+        picked = const.tile([P, P], F32)
+        nc.gpsimd.memset(picked[:], 0.0)
         ident = const.tile([P, P], F32)
         make_identity(nc, ident[:])
+        ident_bf = const.tile([P, P], BF16)
+        make_identity(nc, ident_bf[:])
 
         small_rows = const.tile([P, PACK * P], BF16)
-        nc.vector.memset(small_rows[:], 0.0)
         qw_rows = q2_qw.rearrange("d (s p) a b -> (d s) (p a b)", p=P)
-        nc.sync.dma_start(out=small_rows[0 : DEPTH * SLICES, :], in_=qw_rows)
-        nc.sync.dma_start(out=small_rows[64:96, :], in_=qw_rows[0:32, :])
-        nc.sync.dma_start(out=small_rows[96:112, 0:P], in_=q2_cb.rearrange("(s p) -> s p", p=P))
+        zero = const.tile([P, 1], F32)
+        nc.vector.memset(zero[:], 0.0)
+        table_warmer = const.tile([P, 2], F32)
+        with tc.manual_schedule():
+            nc.sync.dma_start(out=small_rows[0:32, :], in_=qw_rows[0:32, :])
+            nc.sync.dma_start(out=small_rows[32:48, :], in_=qw_rows[32:48, :])
+            nc.sync.dma_start(out=small_rows[64:96, :], in_=qw_rows[0:32, :])
+            nc.sync.dma_start(out=small_rows[96:112, 0:P], in_=q2_cb.rearrange("(s p) -> s p", p=P))
+            nc.scalar.activation(out=table_warmer[:, 0:1], in_=zero[:], func=ACT.Sin)
 
         raw = {}
 
@@ -80,8 +90,6 @@ def tile_quantumneuralnetwork_pb_kernel(tc, h3, q2_qw, q2_cw, q2_cb, w3, b3, out
                     out=raw[c][:], in_=w3[g * K_PASS : (g + 1) * K_PASS, :].rearrange("(t q) o -> q t o", t=PACK)
                 )
 
-        for c in range(0):
-            load(c)
         h3_rows = []
         for i in range(BATCH_SLICES):
             x = const.tile([P, HIDDEN], BF16, name="h3_rows%d" % i)
@@ -95,17 +103,37 @@ def tile_quantumneuralnetwork_pb_kernel(tc, h3, q2_qw, q2_cw, q2_cb, w3, b3, out
         b3_all = const.tile([P, D_OUT], BF16)
         staged = {}
 
-        def stage_in(n):
+        def rows_of(n):
             kind, part, g = units[n]
             if kind == "cw":
-                rows = raw[part * PASSES + g][:]
-            else:
-                rows = raw[CW_CHUNKS + g][:, :, part * BANK : (part + 1) * BANK]
+                return raw[part * PASSES + g][:]
+            return raw[CW_CHUNKS + g][:, :, part * BANK : (part + 1) * BANK]
+
+        flipped = {}
+
+        def flip(n):
+            flipped[n] = []
+            for first in range(0, FLIP[n], 2 * P):
+                bank = psum.tile([P, 2 * BANK], BF16, tag="bank", name="flipped")
+                for i in range(2):
+                    at = first + i * P
+                    nc.tensor.matmul(
+                        bank[:, i * BANK : (i + 1) * BANK].rearrange("p (c t) -> p t c", t=PACK),
+                        lhsT=ident_bf[:], rhs=rows_of(n)[:, :, at : at + P], start=True, stop=True,
+                    )
+                flipped[n].append(bank)
+
+        def stage_in(n):
+            rows = rows_of(n)
             width = rows.shape[2]
-            split = width * VECTOR_SIXTEENTHS // 16
+            start, split = FLIP[n], FLIP[n] + VECTOR[n]
             grouped = grouped_pool.tile([P, width, PACK], BF16, name="grouped", align_bytes=64)
-            regroup(nc.vector.tensor_copy, grouped[:, 0:split, :], rows[:, :, 0:split])
+            regroup(nc.vector.tensor_copy, grouped[:, start:split, :], rows[:, :, start:split])
             regroup(nc.scalar.copy, grouped[:, split:width, :], rows[:, :, split:width])
+            for i, bank in enumerate(flipped[n]):
+                nc.scalar.copy(
+                    out=grouped[:, 2 * P * i : 2 * P * (i + 1), :].rearrange("p c t -> p (c t)"), in_=bank[:]
+                )
             staged[n] = grouped
             if n < W3_CHUNKS:
                 load(CW_CHUNKS + n)
@@ -121,83 +149,85 @@ def tile_quantumneuralnetwork_pb_kernel(tc, h3, q2_qw, q2_cw, q2_cb, w3, b3, out
             )
             return codes, scales
 
-        for n in range(0):
-            stage_in(n)
-
-        entries = small_rows[:].rearrange("r (p e) -> r p e", e=PACK)
-        picked = const.tile([P, P], F32)
-        nc.vector.tensor_copy(out=picked[0:64, :], in_=entries[0:64, :, 0])
-        nc.vector.tensor_copy(out=picked[64:96, :], in_=entries[64:96, :, 3])
-        nc.vector.tensor_copy(out=picked[96:128, :], in_=small_rows[96:128, 0:P])
-        by_unit = psum.tile([P, BANK], F32, tag="bank")
-        nc.tensor.transpose(by_unit[:, 0:P], picked[:], ident[:])
         PHI = 64
         CB = 96
-
         turns = const.tile([P, 2, CB], F32)
-        for f, quarter in enumerate((0.0, 0.25)):
-            nc.vector.tensor_scalar(
-                out=turns[:, f, :], in0=by_unit[:, 0:CB],
-                scalar1=1.0 / (2.0 * math.pi), scalar2=quarter, op0=ALU.mult, op1=ALU.add,
-            )
-        whole_int = const.tile([P, 2, CB], I32)
-        nc.vector.tensor_copy(out=whole_int[:], in_=turns[:])
-        whole = const.tile([P, 2, CB], F32)
-        nc.vector.tensor_copy(out=whole[:], in_=whole_int[:])
+        whole = const.tile([P, 2, CB], I32)
         rest = const.tile([P, 2, CB], F32)
-        nc.vector.tensor_sub(out=rest[:], in0=turns[:], in1=whole[:])
-        flipped = const.tile([P, 2, CB], F32)
-        nc.vector.scalar_tensor_tensor(
-            out=flipped[:], in0=rest[:], scalar=0.5, in1=rest[:], op0=ALU.is_gt, op1=ALU.subtract
-        )
-        folded = const.tile([P, 2, CB], F32)
-        nc.vector.scalar_tensor_tensor(
-            out=folded[:], in0=flipped[:], scalar=0.5, in1=flipped[:], op0=ALU.is_gt, op1=ALU.subtract
-        )
         trig = const.tile([P, 2, CB], F32)
-        nc.scalar.activation(out=trig[:], in_=folded[:], func=ACT.Sin, scale=2.0 * math.pi)
-        table_warmer = const.tile([P, 1], F32)
-        nc.scalar.activation(out=table_warmer[:], in_=trig[:, 0, 0:1], func=ACT.Tanh)
-
-        amp = const.tile([P, 2, 2, SLICES], F32)
-        nc.vector.memset(amp[:], 0.0)
-        nc.vector.memset(amp[:, 0, 0, :], 1.0)
-        for d in range(DEPTH):
-            theta = slice(d * SLICES, (d + 1) * SLICES)
-            by_sin = small.tile([P, 2, 2, SLICES], F32)
-            by_cos = small.tile([P, 2, 2, SLICES], F32)
-            for f, product in enumerate((by_sin, by_cos)):
-                nc.vector.tensor_mul(
-                    out=product[:].rearrange("p a c s -> p (a c) s"),
-                    in0=amp[:].rearrange("p a c s -> p (a c) s"),
-                    in1=trig[:, f, theta].unsqueeze(1).to_broadcast([P, 4, SLICES]),
-                )
-            turned = small.tile([P, 2, 2, SLICES], F32)
-            nc.vector.tensor_sub(out=turned[:, 0], in0=by_cos[:, 0], in1=by_sin[:, 1])
-            nc.vector.tensor_add(out=turned[:, 1], in0=by_sin[:, 0], in1=by_cos[:, 1])
-            if d < DEPTH - 1:
-                phi = slice(PHI + d * SLICES, PHI + (d + 1) * SLICES)
-                ph_sin = small.tile([P, 2, SLICES], F32)
-                ph_cos = small.tile([P, 2, SLICES], F32)
-                for f, product in enumerate((ph_sin, ph_cos)):
-                    nc.vector.tensor_mul(
-                        out=product[:],
-                        in0=turned[:, 1],
-                        in1=trig[:, f, phi].unsqueeze(1).to_broadcast([P, 2, SLICES]),
-                    )
-                nc.vector.tensor_sub(out=turned[:, 1, 0, :], in0=ph_cos[:, 0, :], in1=ph_sin[:, 1, :])
-                nc.vector.tensor_add(out=turned[:, 1, 1, :], in0=ph_sin[:, 0, :], in1=ph_cos[:, 1, :])
-            amp = turned
-        squares = small.tile([P, 2, SLICES], F32)
-        nc.vector.tensor_mul(out=squares[:], in0=amp[:, 0], in1=amp[:, 0])
-        prob = small.tile([P, SLICES], F32)
-        nc.vector.tensor_add(out=prob[:], in0=squares[:, 0, :], in1=squares[:, 1, :])
         hidden_bias = const.tile([P, SLICES], F32)
-        nc.vector.tensor_add(out=hidden_bias[:], in0=prob[:], in1=by_unit[:, CB : CB + SLICES])
+        cb_half = const.tile([P, SLICES], F32)
+        angles = {}
+
+        def pick_angles():
+            by_unit = psum.tile([P, BANK], F32, tag="bank", name="by_unit")
+            angles[0] = by_unit
+            entries = small_rows[:].rearrange("r (p e) -> r p e", e=PACK)
+            nc.vector.tensor_copy(out=picked[0:48, :], in_=entries[0:48, :, 0])
+            nc.vector.tensor_scalar_mul(out=picked[64:96, :], in0=entries[64:96, :, 3], scalar1=0.5)
+            nc.vector.tensor_scalar_add(out=picked[96:112, :], in0=small_rows[96:112, 0:P], scalar1=0.5)
+            nc.tensor.transpose(by_unit[:, 0:P], picked[:], ident[:])
+
+        def sines():
+            by_unit = angles[0]
+            for f, quarter in enumerate((0.0, 0.25)):
+                nc.vector.tensor_scalar(
+                    out=turns[:, f, :], in0=by_unit[:, 0:CB],
+                    scalar1=1.0 / math.pi, scalar2=quarter, op0=ALU.mult, op1=ALU.add,
+                )
+            nc.vector.tensor_copy(out=whole[:], in_=turns[:])
+            nc.vector.tensor_sub(out=rest[:], in0=turns[:], in1=whole[:])
+            nc.vector.tensor_copy(out=cb_half[:], in_=by_unit[:, CB : CB + SLICES])
+            nc.scalar.activation(out=trig[:], in_=rest[:], func=ACT.Sin, scale=2.0 * math.pi)
+
+        def load_tanh_table():
+            nc.scalar.activation(out=table_warmer[:, 1:2], in_=trig[:, 0, 0:1], func=ACT.Tanh)
+
+        def angle(c):
+            return trig[:, :, c : c + SLICES]
+
+        def both(row):
+            return row.unsqueeze(1).to_broadcast([P, 2, SLICES])
+
+        phi_1 = slice(PHI + SLICES, PHI + 2 * SLICES)
+        theta_2 = slice(2 * SLICES, 3 * SLICES)
+        mul, add, sub = nc.vector.tensor_mul, nc.vector.tensor_add, nc.vector.tensor_sub
+        yx = const.tile([P, 2, SLICES], F32)
+        by_z = const.tile([P, 2, SLICES], F32)
+        by_x = const.tile([P, 2, SLICES], F32)
+        y_sin = const.tile([P, SLICES], F32)
+        x = const.tile([P, SLICES], F32)
+        z = const.tile([P, SLICES], F32)
+        x_cos = const.tile([P, SLICES], F32)
+        z_cos = const.tile([P, SLICES], F32)
+        x_last = const.tile([P, SLICES], F32)
+        x_sin = const.tile([P, SLICES], F32)
+        z_last = const.tile([P, SLICES], F32)
+        rotation = [
+            lambda: mul(out=yx[:], in0=angle(PHI), in1=both(trig[:, 0, 0:SLICES])),
+            lambda: mul(out=by_z[:], in0=angle(SLICES), in1=both(trig[:, 1, 0:SLICES])),
+            lambda: mul(out=by_x[:], in0=angle(SLICES), in1=both(yx[:, 1, :])),
+            lambda: mul(out=y_sin[:], in0=yx[:, 0, :], in1=trig[:, 0, phi_1]),
+            lambda: add(out=x[:], in0=by_z[:, 0, :], in1=by_x[:, 1, :]),
+            lambda: sub(out=z[:], in0=by_z[:, 1, :], in1=by_x[:, 0, :]),
+            lambda: mul(out=x_cos[:], in0=x[:], in1=trig[:, 1, phi_1]),
+            lambda: mul(out=z_cos[:], in0=z[:], in1=trig[:, 1, theta_2]),
+            lambda: sub(out=x_last[:], in0=x_cos[:], in1=y_sin[:]),
+            lambda: mul(out=x_sin[:], in0=x_last[:], in1=trig[:, 0, theta_2]),
+            lambda: sub(out=z_last[:], in0=z_cos[:], in1=x_sin[:]),
+            lambda: nc.vector.scalar_tensor_tensor(
+                out=hidden_bias[:], in0=z_last[:], scalar=0.5, in1=cb_half[:],
+                op0=ALU.mult, op1=ALU.add,
+            ),
+        ]
+
+        def rotate(first, last):
+            for step in rotation[first:last]:
+                step()
 
         h3_grouped = const.tile([P, PASSES * BATCH * PACK], BF16, align_bytes=64)
         h3_grouped_words = h3_grouped[:].bitcast(F32).rearrange("q (g b u) -> q g b u", g=PASSES, u=2)
-        for i in range(BATCH_SLICES):
+        def turn_h3(i):
             words = h3_rows[i][:].bitcast(F32)
             for pair in range(PASSES // 2):
                 flipped_words = psum.tile([P, BANK], F32, tag="bank")
@@ -213,7 +243,8 @@ def tile_quantumneuralnetwork_pb_kernel(tc, h3, q2_qw, q2_cw, q2_cb, w3, b3, out
                 )
         h3_codes = const.tile([P, PASSES * BATCH], U32, align_bytes=64)
         h3_scales = const.tile([P, PASSES * BATCH], U8, align_bytes=64)
-        for g in range(PASSES):
+
+        def quantise_h3(g):
             nc.vector.quantize_mx(
                 out=h3_codes[:, g * BATCH : (g + 1) * BATCH].bitcast(FP8X4),
                 scales=h3_scales[:, g * BATCH : (g + 1) * BATCH],
@@ -292,8 +323,37 @@ def tile_quantumneuralnetwork_pb_kernel(tc, h3, q2_qw, q2_cw, q2_cb, w3, b3, out
         def closes(n, kind):
             return 0 <= n < len(units) and units[n][0] == kind and units[n][2] == PASSES - 1
 
-        for n in range(0 - 1, len(units) + 2):
+        with tc.manual_schedule():
+            pick_angles()
+            sines()
+            turn_h3(0)
+            rotate(0, 4)
+            turn_h3(1)
+            rotate(4, 6)
+            turn_h3(2)
+            rotate(6, 8)
+            turn_h3(3)
+            load_tanh_table()
+            rotate(8, 9)
+            quantise_h3(0)
+            rotate(9, 10)
+            quantise_h3(1)
+            rotate(10, 11)
+            quantise_h3(2)
+            rotate(11, 12)
+            quantise_h3(3)
+            flip(0)
+            stage_in(0)
+            flip(1)
+            stage_in(1)
+            multiply(0)
+            flip(2)
+            stage_in(2)
+            multiply(1)
+
+        for n in range(2, len(units) + 2):
             if n + 1 < len(units):
+                flip(n + 1)
                 stage_in(n + 1)
             if closes(n - 1, "cw"):
                 tanh_half(units[n - 1][1])

@@ -29,7 +29,7 @@ CW_CHUNKS = PASSES * (HIDDEN // CHUNK)
 W3_CHUNKS = PASSES * (D_OUT // CHUNK)
 RUN = 4
 FLIP = [0] * 16
-VECTOR = [544] * 8 + [272] * 8
+VECTOR = [480] * 8 + [240] * 8
 
 
 def regroup(copy, grouped, rows):

@@ -28,8 +28,7 @@ CHUNK = 1024
 CW_CHUNKS = PASSES * (HIDDEN // CHUNK)
 W3_CHUNKS = PASSES * (D_OUT // CHUNK)
 RUN = 4
-FLIP = [0] * 16
-VECTOR = [480] * 8 + [240] * 8
+VECTOR_32NDS = 15
 
 
 def regroup(copy, grouped, rows):
@@ -55,8 +54,6 @@ def tile_quantumneuralnetwork_pb_kernel(tc, h3, q2_qw, q2_cw, q2_cb, w3, b3, out
         nc.gpsimd.memset(picked[:], 0.0)
         ident = const.tile([P, P], F32)
         make_identity(nc, ident[:])
-        ident_bf = const.tile([P, P], BF16)
-        make_identity(nc, ident_bf[:])
 
         small_rows = const.tile([P, PACK * P], BF16)
         qw_rows = q2_qw.rearrange("d (s p) a b -> (d s) (p a b)", p=P)
@@ -99,7 +96,8 @@ def tile_quantumneuralnetwork_pb_kernel(tc, h3, q2_qw, q2_cw, q2_cb, w3, b3, out
             load(c)
 
         units = [("cw", half, g) for half in range(HIDDEN // CHUNK) for g in range(PASSES)]
-        units += [("w3", o, g) for o in range(D_OUT // BANK) for g in range(PASSES)]
+        units += [("w3", (0, 1), g) for g in range(2)]
+        units += [("w3", (o,), g) for o in range(D_OUT // BANK) for g in range(2, PASSES)]
         b3_all = const.tile([P, D_OUT], BF16)
         staged = {}
 
@@ -107,33 +105,15 @@ def tile_quantumneuralnetwork_pb_kernel(tc, h3, q2_qw, q2_cw, q2_cb, w3, b3, out
             kind, part, g = units[n]
             if kind == "cw":
                 return raw[part * PASSES + g][:]
-            return raw[CW_CHUNKS + g][:, :, part * BANK : (part + 1) * BANK]
-
-        flipped = {}
-
-        def flip(n):
-            flipped[n] = []
-            for first in range(0, FLIP[n], 2 * P):
-                bank = psum.tile([P, 2 * BANK], BF16, tag="bank", name="flipped")
-                for i in range(2):
-                    at = first + i * P
-                    nc.tensor.matmul(
-                        bank[:, i * BANK : (i + 1) * BANK].rearrange("p (c t) -> p t c", t=PACK),
-                        lhsT=ident_bf[:], rhs=rows_of(n)[:, :, at : at + P], start=True, stop=True,
-                    )
-                flipped[n].append(bank)
+            return raw[CW_CHUNKS + g][:, :, part[0] * BANK : (part[-1] + 1) * BANK]
 
         def stage_in(n):
             rows = rows_of(n)
             width = rows.shape[2]
-            start, split = FLIP[n], FLIP[n] + VECTOR[n]
+            split = width * VECTOR_32NDS // 32
             grouped = grouped_pool.tile([P, width, PACK], BF16, name="grouped", align_bytes=64)
-            regroup(nc.vector.tensor_copy, grouped[:, start:split, :], rows[:, :, start:split])
+            regroup(nc.vector.tensor_copy, grouped[:, 0:split, :], rows[:, :, 0:split])
             regroup(nc.scalar.copy, grouped[:, split:width, :], rows[:, :, split:width])
-            for i, bank in enumerate(flipped[n]):
-                nc.scalar.copy(
-                    out=grouped[:, 2 * P * i : 2 * P * (i + 1), :].rearrange("p c t -> p (c t)"), in_=bank[:]
-                )
             staged[n] = grouped
             if n < W3_CHUNKS:
                 load(CW_CHUNKS + n)
@@ -236,7 +216,7 @@ def tile_quantumneuralnetwork_pb_kernel(tc, h3, q2_qw, q2_cw, q2_cb, w3, b3, out
                     nc.tensor.transpose(
                         flipped_words[:, j * P : (j + 1) * P], words[:, block * P : (block + 1) * P], ident[:]
                     )
-                copy = (nc.scalar.copy, nc.vector.tensor_copy)[pair]
+                copy = nc.vector.tensor_copy if pair == 1 or i == 0 else nc.scalar.copy
                 copy(
                     out=h3_grouped_words[:, 2 * pair : 2 * pair + 2, i * P : (i + 1) * P, :],
                     in_=flipped_words[:].rearrange("q (g u b) -> q g b u", g=2, u=2),
@@ -272,16 +252,18 @@ def tile_quantumneuralnetwork_pb_kernel(tc, h3, q2_qw, q2_cw, q2_cb, w3, b3, out
                         start=first, stop=last,
                     )
             else:
-                for i in range(BATCH_SLICES):
-                    if first:
-                        sums[(part, i)] = psum.tile([P, BANK], F32, tag="bank", name="out_sum%d" % i)
-                    rows = slice(g * BATCH + i * P, g * BATCH + (i + 1) * P)
-                    nc.tensor.matmul_mx(
-                        out=sums[(part, i)][:],
-                        lhsT=h4_codes[:, rows].bitcast(FP8X4), lhsT_scale=h4_scales[:, rows],
-                        rhs=codes[:].bitcast(FP8X4), rhs_scale=scales[:],
-                        start=first, stop=last,
-                    )
+                for o in part:
+                    outs = slice((o - part[0]) * BANK, (o - part[0] + 1) * BANK)
+                    for i in range(BATCH_SLICES):
+                        if first:
+                            sums[(o, i)] = psum.tile([P, BANK], F32, tag="bank", name="out_sum%d" % i)
+                        rows = slice(g * BATCH + i * P, g * BATCH + (i + 1) * P)
+                        nc.tensor.matmul_mx(
+                            out=sums[(o, i)][:],
+                            lhsT=h4_codes[:, rows].bitcast(FP8X4), lhsT_scale=h4_scales[:, rows],
+                            rhs=codes[:, outs].bitcast(FP8X4), rhs_scale=scales[:, outs],
+                            start=first, stop=last,
+                        )
 
         h4_rows = {}
 
@@ -306,19 +288,27 @@ def tile_quantumneuralnetwork_pb_kernel(tc, h3, q2_qw, q2_cw, q2_cb, w3, b3, out
 
         results = {}
 
+        def pieces(o, i):
+            width = BANK // 2 if (o, i) == (1, BATCH_SLICES - 1) else BANK
+            return [slice(at, at + width) for at in range(0, BANK, width)]
+
         def add_b3(o):
             for i in range(BATCH_SLICES):
                 results[(o, i)] = out_pool.tile([P, BANK], F32, name="result")
-                nc.vector.tensor_add(
-                    out=results[(o, i)][:], in0=sums[(o, i)][:], in1=b3_all[:, o * BANK : (o + 1) * BANK]
-                )
+                for cols in pieces(o, i):
+                    nc.vector.tensor_add(
+                        out=results[(o, i)][:, cols], in0=sums[(o, i)][:, cols],
+                        in1=b3_all[:, o * BANK + cols.start : o * BANK + cols.stop],
+                    )
 
         def relu_and_store(o):
             for i in range(BATCH_SLICES):
-                nc.scalar.activation(out=results[(o, i)][:], in_=results[(o, i)][:], func=ACT.Relu)
-                nc.sync.dma_start(
-                    out=out[i * P : (i + 1) * P, o * BANK : (o + 1) * BANK], in_=results[(o, i)][:]
-                )
+                for cols in pieces(o, i):
+                    tile = results[(o, i)][:, cols]
+                    nc.scalar.activation(out=tile, in_=tile, func=ACT.Relu)
+                    nc.sync.dma_start(
+                        out=out[i * P : (i + 1) * P, o * BANK + cols.start : o * BANK + cols.stop], in_=tile
+                    )
 
         def closes(n, kind):
             return 0 <= n < len(units) and units[n][0] == kind and units[n][2] == PASSES - 1
@@ -326,6 +316,7 @@ def tile_quantumneuralnetwork_pb_kernel(tc, h3, q2_qw, q2_cw, q2_cb, w3, b3, out
         with tc.manual_schedule():
             pick_angles()
             sines()
+            load_tanh_table()
             turn_h3(0)
             rotate(0, 4)
             turn_h3(1)
@@ -333,7 +324,6 @@ def tile_quantumneuralnetwork_pb_kernel(tc, h3, q2_qw, q2_cw, q2_cb, w3, b3, out
             turn_h3(2)
             rotate(6, 8)
             turn_h3(3)
-            load_tanh_table()
             rotate(8, 9)
             quantise_h3(0)
             rotate(9, 10)
@@ -342,18 +332,14 @@ def tile_quantumneuralnetwork_pb_kernel(tc, h3, q2_qw, q2_cw, q2_cb, w3, b3, out
             quantise_h3(2)
             rotate(11, 12)
             quantise_h3(3)
-            flip(0)
             stage_in(0)
-            flip(1)
             stage_in(1)
             multiply(0)
-            flip(2)
             stage_in(2)
             multiply(1)
 
         for n in range(2, len(units) + 2):
             if n + 1 < len(units):
-                flip(n + 1)
                 stage_in(n + 1)
             if closes(n - 1, "cw"):
                 tanh_half(units[n - 1][1])

import math
from contextlib import ExitStack

import concourse.mybir as mybir
from concourse.masks import make_identity

F32 = mybir.dt.float32
BF16 = mybir.dt.bfloat16
I32 = mybir.dt.int32
U32 = mybir.dt.uint32
U8 = mybir.dt.uint8
FP8X4 = mybir.dt.float8_e4m3fn_x4
ACT = mybir.ActivationFunctionType
ALU = mybir.AluOpType

BATCH, HIDDEN, D_OUT, DEPTH = 512, 2048, 1024, 3
FLOPS = 2 * BATCH * HIDDEN * HIDDEN + 2 * BATCH * HIDDEN * D_OUT

P = 128
PACK = 4
K_PASS = P * PACK
PASSES = HIDDEN // K_PASS
BANK = 512
BANKS = 8
SLICES = HIDDEN // P
BATCH_SLICES = BATCH // P
CHUNK = 1024
CW_CHUNKS = PASSES * (HIDDEN // CHUNK)
W3_CHUNKS = PASSES * (D_OUT // CHUNK)
RUN = 4
VECTOR_32NDS = 15


def regroup(copy, grouped, rows):
    copy(
        out=grouped.rearrange("p (c i) t -> p c t i", i=RUN),
        in_=rows.rearrange("p t (c i) -> p c t i", i=RUN),
    )


def tile_quantumneuralnetwork_pb_kernel(tc, h3, q2_qw, q2_cw, q2_cb, w3, b3, out):
    nc = tc.nc
    with ExitStack() as ctx:
        const = ctx.enter_context(tc.tile_pool(name="const", bufs=1))
        small = ctx.enter_context(tc.tile_pool(name="small", bufs=2))
        raw_pool = ctx.enter_context(tc.tile_pool(name="raw", bufs=CW_CHUNKS))
        grouped_pool = ctx.enter_context(tc.tile_pool(name="grouped", bufs=3))
        codes_pool = ctx.enter_context(tc.tile_pool(name="codes", bufs=3))
        h4_pool = ctx.enter_context(tc.tile_pool(name="h4", bufs=2))
        out_pool = ctx.enter_context(tc.tile_pool(name="outs", bufs=8))
        psum = ctx.enter_context(tc.psum_pool(name="psum", bufs=BANKS))

        picked = const.tile([P, P], F32)
        nc.gpsimd.memset(picked[:], 0.0)
        ident = const.tile([P, P], F32)
        make_identity(nc, ident[:])

        small_rows = const.tile([P, PACK * P], BF16)
        qw_rows = q2_qw.rearrange("d (s p) a b -> (d s) (p a b)", p=P)
        zero = const.tile([P, 1], F32)
        nc.vector.memset(zero[:], 0.0)
        table_warmer = const.tile([P, 2], F32)
        with tc.manual_schedule():
            nc.sync.dma_start(out=small_rows[0:32, :], in_=qw_rows[0:32, :])
            nc.sync.dma_start(out=small_rows[32:48, :], in_=qw_rows[32:48, :])
            nc.sync.dma_start(out=small_rows[64:96, :], in_=qw_rows[0:32, :])
            nc.sync.dma_start(out=small_rows[96:112, 0:P], in_=q2_cb.rearrange("(s p) -> s p", p=P))
            nc.scalar.activation(out=table_warmer[:, 0:1], in_=zero[:], func=ACT.Sin)

        raw = {}

        def load(c):
            raw[c] = raw_pool.tile([P, PACK, CHUNK], BF16, name="raw")
            if c < CW_CHUNKS:
                half, g = divmod(c, PASSES)
                for u in range(2):
                    first = g * K_PASS + u * 2 * P
                    nc.sync.dma_start(
                        out=raw[c][:, 2 * u : 2 * u + 2, :],
                        in_=q2_cw[first : first + 2 * P, half * CHUNK : (half + 1) * CHUNK].rearrange(
                            "(q e) n -> q e n", e=2
                        ),
                    )
            else:
                g = c - CW_CHUNKS
                nc.sync.dma_start(
                    out=raw[c][:], in_=w3[g * K_PASS : (g + 1) * K_PASS, :].rearrange("(t q) o -> q t o", t=PACK)
                )

        h3_rows = []
        for i in range(BATCH_SLICES):
            x = const.tile([P, HIDDEN], BF16, name="h3_rows%d" % i)
            nc.sync.dma_start(out=x[:], in_=h3[i * P : (i + 1) * P, :])
            h3_rows.append(x)
        for c in range(0, CW_CHUNKS):
            load(c)

        units = [("cw", half, g) for half in range(HIDDEN // CHUNK) for g in range(PASSES)]
        units += [("w3", (0, 1), g) for g in range(2)]
        units += [("w3", (o,), g) for o in range(D_OUT // BANK) for g in range(2, PASSES)]
        b3_all = const.tile([P, D_OUT], BF16)
        staged = {}

        def rows_of(n):
            kind, part, g = units[n]
            if kind == "cw":
                return raw[part * PASSES + g][:]
            return raw[CW_CHUNKS + g][:, :, part[0] * BANK : (part[-1] + 1) * BANK]

        def stage_in(n):
            rows = rows_of(n)
            width = rows.shape[2]
            split = width * VECTOR_32NDS // 32
            grouped = grouped_pool.tile([P, width, PACK], BF16, name="grouped", align_bytes=64)
            regroup(nc.vector.tensor_copy, grouped[:, 0:split, :], rows[:, :, 0:split])
            regroup(nc.scalar.copy, grouped[:, split:width, :], rows[:, :, split:width])
            staged[n] = grouped
            if n < W3_CHUNKS:
                load(CW_CHUNKS + n)
            if n == W3_CHUNKS:
                nc.sync.dma_start(out=b3_all[:], in_=b3.partition_broadcast(P))

        def quantise_unit(n):
            width = staged[n].shape[1]
            codes = codes_pool.tile([P, width], U32, name="codes", align_bytes=64)
            scales = codes_pool.tile([P, width], U8, name="scales", align_bytes=64)
            nc.vector.quantize_mx(
                out=codes[:].bitcast(FP8X4), scales=scales[:], in_=staged[n][:].rearrange("p c t -> p (c t)")
            )
            return codes, scales

        PHI = 64
        CB = 96
        turns = const.tile([P, 2, CB], F32)
        whole = const.tile([P, 2, CB], I32)
        rest = const.tile([P, 2, CB], F32)
        trig = const.tile([P, 2, CB], F32)
        hidden_bias = const.tile([P, SLICES], F32)
        cb_half = const.tile([P, SLICES], F32)
        angles = {}

        def pick_angles():
            by_unit = psum.tile([P, BANK], F32, tag="bank", name="by_unit")
            angles[0] = by_unit
            entries = small_rows[:].rearrange("r (p e) -> r p e", e=PACK)
            nc.vector.tensor_copy(out=picked[0:48, :], in_=entries[0:48, :, 0])
            nc.vector.tensor_scalar_mul(out=picked[64:96, :], in0=entries[64:96, :, 3], scalar1=0.5)
            nc.vector.tensor_scalar_add(out=picked[96:112, :], in0=small_rows[96:112, 0:P], scalar1=0.5)
            nc.tensor.transpose(by_unit[:, 0:P], picked[:], ident[:])

        def sines():
            by_unit = angles[0]
            for f, quarter in enumerate((0.0, 0.25)):
                nc.vector.tensor_scalar(
                    out=turns[:, f, :], in0=by_unit[:, 0:CB],
                    scalar1=1.0 / math.pi, scalar2=quarter, op0=ALU.mult, op1=ALU.add,
                )
            nc.vector.tensor_copy(out=whole[:], in_=turns[:])
            nc.vector.tensor_sub(out=rest[:], in0=turns[:], in1=whole[:])
            nc.vector.tensor_copy(out=cb_half[:], in_=by_unit[:, CB : CB + SLICES])
            nc.scalar.activation(out=trig[:], in_=rest[:], func=ACT.Sin, scale=2.0 * math.pi)

        def load_tanh_table():
            nc.scalar.activation(out=table_warmer[:, 1:2], in_=trig[:, 0, 0:1], func=ACT.Tanh)

        def angle(c):
            return trig[:, :, c : c + SLICES]

        def both(row):
            return row.unsqueeze(1).to_broadcast([P, 2, SLICES])

        phi_1 = slice(PHI + SLICES, PHI + 2 * SLICES)
        theta_2 = slice(2 * SLICES, 3 * SLICES)
        mul, add, sub = nc.vector.tensor_mul, nc.vector.tensor_add, nc.vector.tensor_sub
        yx = const.tile([P, 2, SLICES], F32)
        by_z = const.tile([P, 2, SLICES], F32)
        by_x = const.tile([P, 2, SLICES], F32)
        y_sin = const.tile([P, SLICES], F32)
        x = const.tile([P, SLICES], F32)
        z = const.tile([P, SLICES], F32)
        x_cos = const.tile([P, SLICES], F32)
        z_cos = const.tile([P, SLICES], F32)
        x_last = const.tile([P, SLICES], F32)
        x_sin = const.tile([P, SLICES], F32)
        z_last = const.tile([P, SLICES], F32)
        rotation = [
            lambda: mul(out=yx[:], in0=angle(PHI), in1=both(trig[:, 0, 0:SLICES])),
            lambda: mul(out=by_z[:], in0=angle(SLICES), in1=both(trig[:, 1, 0:SLICES])),
            lambda: mul(out=by_x[:], in0=angle(SLICES), in1=both(yx[:, 1, :])),
            lambda: mul(out=y_sin[:], in0=yx[:, 0, :], in1=trig[:, 0, phi_1]),
            lambda: add(out=x[:], in0=by_z[:, 0, :], in1=by_x[:, 1, :]),
            lambda: sub(out=z[:], in0=by_z[:, 1, :], in1=by_x[:, 0, :]),
            lambda: mul(out=x_cos[:], in0=x[:], in1=trig[:, 1, phi_1]),
            lambda: mul(out=z_cos[:], in0=z[:], in1=trig[:, 1, theta_2]),
            lambda: sub(out=x_last[:], in0=x_cos[:], in1=y_sin[:]),
            lambda: mul(out=x_sin[:], in0=x_last[:], in1=trig[:, 0, theta_2]),
            lambda: sub(out=z_last[:], in0=z_cos[:], in1=x_sin[:]),
            lambda: nc.vector.scalar_tensor_tensor(
                out=hidden_bias[:], in0=z_last[:], scalar=0.5, in1=cb_half[:],
                op0=ALU.mult, op1=ALU.add,
            ),
        ]

        def rotate(first, last):
            for step in rotation[first:last]:
                step()

        h3_grouped = const.tile([P, PASSES * BATCH * PACK], BF16, align_bytes=64)
        h3_grouped_words = h3_grouped[:].bitcast(F32).rearrange("q (g b u) -> q g b u", g=PASSES, u=2)
        def turn_h3(i):
            words = h3_rows[i][:].bitcast(F32)
            for pair in range(PASSES // 2):
                flipped_words = psum.tile([P, BANK], F32, tag="bank")
                for j in range(4):
                    block = 4 * pair + j
                    nc.tensor.transpose(
                        flipped_words[:, j * P : (j + 1) * P], words[:, block * P : (block + 1) * P], ident[:]
                    )
                copy = nc.vector.tensor_copy if pair == 1 or i == 0 else nc.scalar.copy
                copy(
                    out=h3_grouped_words[:, 2 * pair : 2 * pair + 2, i * P : (i + 1) * P, :],
                    in_=flipped_words[:].rearrange("q (g u b) -> q g b u", g=2, u=2),
                )
        h3_codes = const.tile([P, PASSES * BATCH], U32, align_bytes=64)
        h3_scales = const.tile([P, PASSES * BATCH], U8, align_bytes=64)

        def quantise_h3(g):
            nc.vector.quantize_mx(
                out=h3_codes[:, g * BATCH : (g + 1) * BATCH].bitcast(FP8X4),
                scales=h3_scales[:, g * BATCH : (g + 1) * BATCH],
                in_=h3_grouped[:, g * BATCH * PACK : (g + 1) * BATCH * PACK],
            )

        h4_codes = const.tile([P, PASSES * BATCH], U32, align_bytes=64)
        h4_scales = const.tile([P, PASSES * BATCH], U8, align_bytes=64)
        sums = {}

        def multiply(n):
            kind, part, g = units[n]
            codes, scales = quantise_unit(n)
            first, last = g == 0, g == PASSES - 1
            if kind == "cw":
                batch = slice(g * BATCH, (g + 1) * BATCH)
                for s in range(BANKS):
                    if first:
                        sums[s] = psum.tile([P, BANK], F32, tag="bank", name="hidden_sum%d" % s)
                    cols = slice(s * P, (s + 1) * P)
                    nc.tensor.matmul_mx(
                        out=sums[s][:],
                        lhsT=codes[:, cols].bitcast(FP8X4), lhsT_scale=scales[:, cols],
                        rhs=h3_codes[:, batch].bitcast(FP8X4), rhs_scale=h3_scales[:, batch],
                        start=first, stop=last,
                    )
            else:
                for o in part:
                    outs = slice((o - part[0]) * BANK, (o - part[0] + 1) * BANK)
                    for i in range(BATCH_SLICES):
                        if first:
                            sums[(o, i)] = psum.tile([P, BANK], F32, tag="bank", name="out_sum%d" % i)
                        rows = slice(g * BATCH + i * P, g * BATCH + (i + 1) * P)
                        nc.tensor.matmul_mx(
                            out=sums[(o, i)][:],
                            lhsT=h4_codes[:, rows].bitcast(FP8X4), lhsT_scale=h4_scales[:, rows],
                            rhs=codes[:, outs].bitcast(FP8X4), rhs_scale=scales[:, outs],
                            start=first, stop=last,
                        )

        h4_rows = {}

        def tanh_half(half):
            for s in range(BANKS):
                g2, t = divmod(half * BANKS + s, PACK)
                if t == 0:
                    h4_rows[g2] = h4_pool.tile([P, PACK, BATCH], BF16, name="h4_rows")
                nc.scalar.activation(
                    out=h4_rows[g2][:, t, :], in_=sums[s][:], func=ACT.Tanh,
                    bias=hidden_bias[:, half * BANKS + s : half * BANKS + s + 1], scale=1.0,
                )

        def quantise_h4(g2):
            h4_grouped = h4_pool.tile([P, BATCH, PACK], BF16, name="h4_grouped", align_bytes=64)
            regroup(nc.vector.tensor_copy, h4_grouped[:], h4_rows[g2][:])
            nc.vector.quantize_mx(
                out=h4_codes[:, g2 * BATCH : (g2 + 1) * BATCH].bitcast(FP8X4),
                scales=h4_scales[:, g2 * BATCH : (g2 + 1) * BATCH],
                in_=h4_grouped[:].rearrange("p b t -> p (b t)"),
            )

        results = {}

        def pieces(o, i):
            width = BANK // 2 if (o, i) == (1, BATCH_SLICES - 1) else BANK
            return [slice(at, at + width) for at in range(0, BANK, width)]

        def add_b3(o):
            for i in range(BATCH_SLICES):
                results[(o, i)] = out_pool.tile([P, BANK], F32, name="result")
                for cols in pieces(o, i):
                    nc.vector.tensor_add(
                        out=results[(o, i)][:, cols], in0=sums[(o, i)][:, cols],
                        in1=b3_all[:, o * BANK + cols.start : o * BANK + cols.stop],
                    )

        def relu_and_store(o):
            for i in range(BATCH_SLICES):
                for cols in pieces(o, i):
                    tile = results[(o, i)][:, cols]
                    nc.scalar.activation(out=tile, in_=tile, func=ACT.Relu)
                    nc.sync.dma_start(
                        out=out[i * P : (i + 1) * P, o * BANK + cols.start : o * BANK + cols.stop], in_=tile
                    )

        def closes(n, kind):
            return 0 <= n < len(units) and units[n][0] == kind and units[n][2] == PASSES - 1

        with tc.manual_schedule():
            pick_angles()
            sines()
            load_tanh_table()
            turn_h3(0)
            rotate(0, 4)
            turn_h3(1)
            rotate(4, 6)
            turn_h3(2)
            rotate(6, 8)
            turn_h3(3)
            rotate(8, 9)
            quantise_h3(0)
            rotate(9, 10)
            quantise_h3(1)
            rotate(10, 11)
            quantise_h3(2)
            rotate(11, 12)
            quantise_h3(3)
            stage_in(0)
            stage_in(1)
            multiply(0)
            stage_in(2)
            multiply(1)

        for n in range(2, len(units) + 2):
            if n + 1 < len(units):
                stage_in(n + 1)
            if closes(n - 1, "cw"):
                tanh_half(units[n - 1][1])
            if closes(n - 2, "cw"):
                quantise_h4(2 * units[n - 2][1])
            if closes(n - 3, "cw"):
                quantise_h4(2 * units[n - 3][1] + 1)
            if 0 <= n < len(units):
                multiply(n)
            if n == len(units) - 1:
                for o in range(D_OUT // BANK):
                    add_b3(o)
                for o in range(D_OUT // BANK):
                    relu_and_store(o)
